import numpy as np
import ml_dtypes


def mxq(x, axis, fmt="e4m3"):
    dtype, down = {"e4m3": (ml_dtypes.float8_e4m3fn, 7), "e5m2": (ml_dtypes.float8_e5m2, 14)}[fmt]
    v = np.moveaxis(np.asarray(x, np.float32).astype(ml_dtypes.bfloat16).astype(np.float64), axis, -1)
    blocks = v.reshape(v.shape[:-1] + (-1, 32))
    amax = np.abs(blocks).max(-1, keepdims=True)
    byte = np.maximum(np.where(amax > 0, np.frexp(amax)[1] - 1 + 127, 0) - down, 1)
    scale = np.exp2(byte - 127.0)
    codes = (blocks / scale).astype(np.float32).astype(dtype).astype(np.float64)
    return np.moveaxis((codes * scale).reshape(v.shape), -1, axis)


WIDE = False


def mx_kscale(k):
    if not WIDE:
        return np.ones(k)
    levels = np.array([10, -10, 5, -5, 0])
    a = np.random.permutation(np.resize(levels, k // 512 * 4)).reshape(k // 512, 4)
    idx = np.arange(k)
    return np.exp2(a[idx // 512, idx % 128 // 32])


BF16 = ml_dtypes.bfloat16


def bf(x):
    return np.asarray(x, np.float32).astype(BF16)


def f64(x):
    return np.asarray(x).astype(np.float64)


B, S, D, H, DH, DR, DKV, DQ = 2, 4096, 512, 2, 128, 64, 512, 1024
HALF = DR // 2


def rope(t, cos, sin):
    t1, t2 = t[..., 0::2], t[..., 1::2]
    c = cos[None, :, None, :]
    s = sin[None, :, None, :]
    return np.stack([t1 * c - t2 * s, t1 * s + t2 * c], axis=-1).reshape(t.shape)


def setup_inputs():
    s, t = mx_kscale(D), mx_kscale(DKV)
    ang = np.random.uniform(0.0, 2.0 * np.pi, (S, HALF))
    return {"x": bf(np.random.standard_normal((B, S, D)) * s),
            "W_kv_down": bf(np.random.standard_normal((D, DKV)) / np.sqrt(D) / s[:, None] * t),
            "W_k_up": bf(np.random.standard_normal((DKV, H * DH)) / np.sqrt(DKV) / t[:, None]),
            "W_v_up": bf(np.random.standard_normal((DKV, H * DH)) / np.sqrt(DKV) / t[:, None]),
            "W_k_rope": bf(np.random.standard_normal((D, H * DR)) / np.sqrt(D) / s[:, None]),
            "rope_cos": bf(np.cos(ang)), "rope_sin": bf(np.sin(ang))}


def reference(x, W_kv_down, W_k_up, W_v_up, W_k_rope, rope_cos, rope_sin):
    xq = mxq(f64(x), 2, "e4m3")
    down_kv = xq @ mxq(f64(W_kv_down), 0, "e4m3")
    dkv = mxq(down_kv, 2, "e4m3")
    k_c = (dkv @ mxq(f64(W_k_up), 0, "e4m3")).reshape(B, S, H, DH)
    v = (dkv @ mxq(f64(W_v_up), 0, "e4m3")).reshape(B, S, H, DH)
    k_r = (xq @ mxq(f64(W_k_rope), 0, "e4m3")).reshape(B, S, H, DR)
    k_r = rope(k_r, f64(rope_cos), f64(rope_sin))
    k = np.concatenate([k_c, k_r], axis=-1).transpose(0, 2, 1, 3)
    return k, v.transpose(0, 2, 1, 3)

@@ -1,0 +1,271 @@
+from contextlib import ExitStack
+
+import concourse.mybir as mybir
+from concourse.masks import make_identity
+
+F32 = mybir.dt.float32
+BF16 = mybir.dt.bfloat16
+U32 = mybir.dt.uint32
+U8 = mybir.dt.uint8
+FP8X4 = mybir.dt.float8_e4m3fn_x4
+MULT = mybir.AluOpType.mult
+ADD = mybir.AluOpType.add
+
+P = 128
+PACK = 4
+BATCH, SEQ, D_MODEL = 2, 4096, 512
+HEADS, D_HEAD, D_ROPE, D_LATENT = 2, 128, 64, 512
+PAIRS = D_ROPE // 2
+D_KEY = D_HEAD + D_ROPE
+POSITIONS = SEQ // P
+CHUNK = 4
+CHUNK_TOKENS = CHUNK * P
+CHUNKS_PER_SEQ = POSITIONS // CHUNK
+N_CHUNKS = BATCH * CHUNKS_PER_SEQ
+UP_COLS = 2 * HEADS * D_HEAD
+ROPE_COLS = HEADS * D_ROPE
+
+assert D_MODEL == P * PACK and D_LATENT == P * PACK
+
+FLOPS = 2 * BATCH * SEQ * (D_MODEL * D_LATENT + D_LATENT * UP_COLS + D_MODEL * ROPE_COLS)
+
+
+def tile_multiheadlatentattention_pb_t_kernel(
+    tc, x, W_kv_down, W_k_up, W_v_up, W_k_rope, rope_cos, rope_sin, out_0, out_1
+):
+    nc = tc.nc
+
+    x_view = x.rearrange("b (p t) d -> b p t d", t=POSITIONS)
+    keys_view = out_0.rearrange("b h (p t) f -> b p h t f", t=POSITIONS)
+    values_view = out_1.rearrange("b h (p t) f -> b p h t f", t=POSITIONS)
+
+    with ExitStack() as ctx:
+        ctx.enter_context(tc.manual_schedule())
+        consts = ctx.enter_context(tc.tile_pool(name="consts", bufs=1))
+        x_pool = ctx.enter_context(tc.tile_pool(name="x_pool", bufs=N_CHUNKS))
+        grouped_pool = ctx.enter_context(tc.tile_pool(name="grouped_pool", bufs=2))
+        codes_pool = ctx.enter_context(tc.tile_pool(name="codes_pool", bufs=3))
+        rope_pool = ctx.enter_context(tc.tile_pool(name="rope_pool", bufs=2))
+        keys_pool = ctx.enter_context(tc.tile_pool(name="keys_pool", bufs=5))
+        values_pool = ctx.enter_context(tc.tile_pool(name="values_pool", bufs=3))
+        psum_xt = ctx.enter_context(tc.psum_pool(name="psum_xt", bufs=2))
+        psum_down = ctx.enter_context(tc.psum_pool(name="psum_down", bufs=2))
+        psum_up = ctx.enter_context(tc.psum_pool(name="psum_up", bufs=3))
+        psum_rope = ctx.enter_context(tc.psum_pool(name="psum_rope", bufs=1))
+
+        x_sb, x_grouped, x_codes, x_scales = {}, {}, {}, {}
+        d_grouped, d_codes, d_scales = {}, {}, {}
+        k_sb, v_sb = {}, {}
+
+        def live(c):
+            return 0 <= c < N_CHUNKS
+
+        def copy_out(piece):
+            return nc.scalar.copy if piece % 2 == 0 else nc.vector.tensor_copy
+
+        def place(c):
+            return c // CHUNKS_PER_SEQ, (c % CHUNKS_PER_SEQ) * CHUNK
+
+        def load_chunk(c):
+            b, first = place(c)
+            x_sb[c] = x_pool.tile([P, CHUNK, D_MODEL], BF16, name="x_sb")
+            nc.sync.dma_start(out=x_sb[c][:], in_=x_view[b, :, first : first + CHUNK, :])
+
+        def quantise(name, grouped, width, pool):
+            codes = pool.tile([P, width], U32, name=name + "_codes", align_bytes=64)
+            scales = pool.tile([P, width], U8, name=name + "_scales", align_bytes=64)
+            nc.vector.quantize_mx(out=codes[:].bitcast(FP8X4), scales=scales[:], in_=grouped)
+            return codes, scales
+
+        wd_raw = consts.tile([P, PACK, D_LATENT], BF16)
+        nc.sync.dma_start(
+            out=wd_raw[:].rearrange("p (u e) n -> p u e n", u=2),
+            in_=W_kv_down.rearrange("(u p e) n -> p u e n", u=2, e=2),
+        )
+        load_chunk(0)
+        wr_raw = consts.tile([P, PACK, ROPE_COLS], BF16)
+        nc.sync.dma_start(
+            out=wr_raw[:].rearrange("p (u e) n -> p u e n", u=2),
+            in_=W_k_rope.rearrange("(u p e) n -> p u e n", u=2, e=2),
+        )
+        load_chunk(1)
+        cos_raw = consts.tile([P, POSITIONS, PAIRS], BF16)
+        nc.sync.dma_start(out=cos_raw[:], in_=rope_cos.rearrange("(p t) i -> p t i", t=POSITIONS))
+        sin_raw = consts.tile([P, POSITIONS, PAIRS], BF16)
+        nc.sync.dma_start(out=sin_raw[:], in_=rope_sin.rearrange("(p t) i -> p t i", t=POSITIONS))
+        load_chunk(2)
+        wup_raw = consts.tile([P, PACK, UP_COLS], BF16)
+        nc.sync.dma_start(out=wup_raw[:, :, 0 : UP_COLS // 2], in_=W_k_up.rearrange("(p t) n -> p t n", t=PACK))
+        nc.sync.dma_start(out=wup_raw[:, :, UP_COLS // 2 : UP_COLS], in_=W_v_up.rearrange("(p t) n -> p t n", t=PACK))
+        for c in range(3, N_CHUNKS):
+            load_chunk(c)
+
+        ident = consts.tile([P, P], F32)
+        make_identity(nc, ident[:])
+
+        def transpose_chunk(c):
+            if not live(c):
+                return
+            x_grouped[c] = grouped_pool.tile([P, CHUNK_TOKENS * PACK], BF16, name="x_grouped", align_bytes=64)
+            grouped_words = x_grouped[c][:].bitcast(F32).rearrange("p (j w u) -> p j w u", j=CHUNK, u=2)
+            for pair in range(CHUNK // 2):
+                x_t = psum_xt.tile([P, 2, 2, P], F32, name="x_t")
+                for j in range(2):
+                    words = x_sb[c][:, 2 * pair + j, :].bitcast(F32)
+                    for u in range(2):
+                        nc.tensor.transpose(x_t[:, j, u, :], words[:, u * P : (u + 1) * P], ident[:])
+                copy_out(pair)(
+                    out=grouped_words[:, 2 * pair : 2 * pair + 2], in_=x_t[:].rearrange("p j u w -> p j w u")
+                )
+
+        def quantise_x(c):
+            if not live(c):
+                return
+            x_codes[c], x_scales[c] = quantise("x", x_grouped[c][:], CHUNK_TOKENS, codes_pool)
+
+        def down(c, j):
+            if not live(c):
+                return
+            if j == 0:
+                d_grouped[c] = grouped_pool.tile([P, CHUNK, P, PACK], BF16, name="d_grouped", align_bytes=64)
+            tokens = slice(j * P, (j + 1) * P)
+            down_t = psum_down.tile([P, PACK, P], F32, name="down_t")
+            for f in range(PACK):
+                cols = slice(f * P, (f + 1) * P)
+                nc.tensor.matmul_mx(
+                    out=down_t[:, f, :],
+                    lhsT=wd_codes[:, cols].bitcast(FP8X4),
+                    lhsT_scale=wd_scales[:, cols],
+                    rhs=x_codes[c][:, tokens].bitcast(FP8X4),
+                    rhs_scale=x_scales[c][:, tokens],
+                    start=True,
+                    stop=True,
+                )
+            nc.scalar.copy(out=d_grouped[c][:, j], in_=down_t[:].rearrange("p f w -> p w f"))
+
+        def quantise_down(c):
+            if not live(c):
+                return
+            d_codes[c], d_scales[c] = quantise(
+                "d", d_grouped[c][:].rearrange("p j w f -> p (j w f)"), CHUNK_TOKENS, codes_pool
+            )
+
+        def rope(c):
+            if not live(c):
+                return
+            first = place(c)[1]
+            k_sb[c] = keys_pool.tile([P, HEADS, CHUNK, D_KEY], F32, name="k_sb")
+            k_r = psum_rope.tile([P, CHUNK, ROPE_COLS], F32, name="k_r")
+            for j in range(CHUNK):
+                tokens = slice(j * P, (j + 1) * P)
+                nc.tensor.matmul_mx(
+                    out=k_r[:, j, :],
+                    lhsT=x_codes[c][:, tokens].bitcast(FP8X4),
+                    lhsT_scale=x_scales[c][:, tokens],
+                    rhs=wr_codes[:].bitcast(FP8X4),
+                    rhs_scale=wr_scales[:],
+                    start=True,
+                    stop=True,
+                )
+            positions = slice(first, first + CHUNK)
+            by_cos = rope_pool.tile([P, HEADS, CHUNK, D_ROPE], F32, name="by_cos")
+            nc.vector.tensor_tensor(
+                out=by_cos[:].rearrange("p h j f -> p j h f"),
+                in0=k_r[:].rearrange("p j (h f) -> p j h f", h=HEADS),
+                in1=cos_twice[:, positions, :].unsqueeze(2).to_broadcast([P, CHUNK, HEADS, D_ROPE]),
+                op=MULT,
+            )
+            by_sin = rope_pool.tile([P, 2, HEADS, CHUNK, PAIRS], F32, name="by_sin")
+            k_r_pairs = k_r[:].rearrange("p j (h i e) -> p j h i e", h=HEADS, e=2)
+            for e, table in ((0, sin_minus), (1, sin_raw)):
+                nc.vector.tensor_tensor(
+                    out=by_sin[:, e].rearrange("p h j i -> p j h i"),
+                    in0=k_r_pairs[:, :, :, :, 1 - e],
+                    in1=table[:, positions, :].unsqueeze(2).to_broadcast([P, CHUNK, HEADS, PAIRS]),
+                    op=MULT,
+                )
+            nc.gpsimd.tensor_tensor(
+                out=k_sb[c][:, :, :, D_HEAD:D_KEY].rearrange("p h j (i e) -> p h j i e", e=2),
+                in0=by_cos[:].rearrange("p h j (i e) -> p h j i e", e=2),
+                in1=by_sin[:].rearrange("p e h j i -> p h j i e"),
+                op=ADD,
+            )
+
+        def up(c, j):
+            if not live(c):
+                return
+            if j == 0:
+                v_sb[c] = values_pool.tile([P, HEADS, CHUNK, D_HEAD], F32, name="v_sb")
+            tokens = slice(j * P, (j + 1) * P)
+            kc_v = psum_up.tile([P, 2, HEADS, D_HEAD], F32, name="kc_v")
+            nc.tensor.matmul_mx(
+                out=kc_v[:].rearrange("p s h f -> p (s h f)"),
+                lhsT=d_codes[c][:, tokens].bitcast(FP8X4),
+                lhsT_scale=d_scales[c][:, tokens],
+                rhs=wup_codes[:].bitcast(FP8X4),
+                rhs_scale=wup_scales[:],
+                start=True,
+                stop=True,
+            )
+            copy_out(j)(out=k_sb[c][:, :, j, 0:D_HEAD], in_=kc_v[:, 0])
+            copy_out(j)(out=v_sb[c][:, :, j, :], in_=kc_v[:, 1])
+
+        def store(c):
+            if not live(c):
+                return
+            b, first = place(c)
+            nc.sync.dma_start(out=keys_view[b, :, :, first : first + CHUNK, :], in_=k_sb[c][:])
+            nc.sync.dma_start(out=values_view[b, :, :, first : first + CHUNK, :], in_=v_sb[c][:])
+
+        def rope_tables(g):
+            positions = slice(g * CHUNK, (g + 1) * CHUNK)
+            nc.gpsimd.tensor_scalar(
+                out=cos_twice[:, positions, :].rearrange("p t (i e) -> p t i e", e=2),
+                in0=cos_raw[:, positions, :].unsqueeze(3).to_broadcast([P, CHUNK, PAIRS, 2]),
+                scalar1=1.0,
+                scalar2=0.0,
+                op0=MULT,
+                op1=ADD,
+            )
+            nc.gpsimd.tensor_scalar(
+                out=sin_minus[:, positions, :], in0=sin_raw[:, positions, :], scalar1=-1.0, scalar2=0.0, op0=MULT, op1=ADD
+            )
+
+        def step(s):
+            quantise_x(s + 2)
+            quantise_down(s)
+            down(s + 1, 0)
+            up(s - 1, 0)
+            down(s + 1, 1)
+            up(s - 1, 1)
+            rope(s + 1)
+            down(s + 1, 2)
+            up(s - 1, 2)
+            transpose_chunk(s + 3)
+            down(s + 1, 3)
+            up(s - 1, 3)
+            store(s - 1)
+
+        wd_grouped = consts.tile([P, PACK, P, PACK], BF16, align_bytes=64)
+        nc.vector.tensor_copy(out=wd_grouped[:], in_=wd_raw[:].rearrange("p t (m f) -> p f m t", f=PACK))
+        wd_codes, wd_scales = quantise("wd", wd_grouped[:].rearrange("p f m t -> p (f m t)"), D_LATENT, consts)
+        wr_grouped = consts.tile([P, ROPE_COLS, PACK], BF16, align_bytes=64)
+        nc.scalar.copy(out=wr_grouped[:], in_=wr_raw[:].rearrange("p t n -> p n t"))
+        step(-3)
+        step(-2)
+        wr_codes, wr_scales = quantise("wr", wr_grouped[:].rearrange("p n t -> p (n t)"), ROPE_COLS, consts)
+        cos_twice = consts.tile([P, POSITIONS, D_ROPE], BF16)
+        sin_minus = consts.tile([P, POSITIONS, PAIRS], BF16)
+        rope_tables(0)
+        rope_tables(1)
+        wup_grouped = consts.tile([P, UP_COLS, PACK], BF16, align_bytes=64)
+        nc.gpsimd.tensor_scalar(
+            out=wup_grouped[:], in0=wup_raw[:].rearrange("p t n -> p n t"), scalar1=1.0, scalar2=0.0, op0=MULT, op1=ADD
+        )
+        for g in range(2, CHUNKS_PER_SEQ):
+            rope_tables(g)
+        step(-1)
+        step(0)
+        wup_codes, wup_scales = quantise("wup", wup_grouped[:].rearrange("p n t -> p (n t)"), UP_COLS, consts)
+        for s in range(1, N_CHUNKS + 1):
+            step(s)

@@ -184,7 +184,7 @@ def tile_multiheadlatentattention_pb_t_kernel(
                     in1=table[:, positions, :].unsqueeze(2).to_broadcast([P, CHUNK, HEADS, PAIRS]),
                     op=MULT,
                 )
-            nc.gpsimd.tensor_tensor(
+            nc.vector.tensor_tensor(
                 out=k_sb[c][:, :, :, D_HEAD:D_KEY].rearrange("p h j (i e) -> p h j i e", e=2),
                 in0=by_cos[:].rearrange("p h j (i e) -> p h j i e", e=2),
                 in1=by_sin[:].rearrange("p e h j i -> p h j i e"),

@@ -13,6 +13,7 @@ ADD = mybir.AluOpType.add
 
 P = 128
 PACK = 4
+PSUM_BANKS = 8
 BATCH, SEQ, D_MODEL = 2, 4096, 512
 HEADS, D_HEAD, D_ROPE, D_LATENT = 2, 128, 64, 512
 PAIRS = D_ROPE // 2
@@ -48,10 +49,7 @@ def tile_multiheadlatentattention_pb_t_kernel(
         rope_pool = ctx.enter_context(tc.tile_pool(name="rope_pool", bufs=2))
         keys_pool = ctx.enter_context(tc.tile_pool(name="keys_pool", bufs=5))
         values_pool = ctx.enter_context(tc.tile_pool(name="values_pool", bufs=3))
-        psum_xt = ctx.enter_context(tc.psum_pool(name="psum_xt", bufs=2))
-        psum_down = ctx.enter_context(tc.psum_pool(name="psum_down", bufs=2))
-        psum_up = ctx.enter_context(tc.psum_pool(name="psum_up", bufs=3))
-        psum_rope = ctx.enter_context(tc.psum_pool(name="psum_rope", bufs=1))
+        psum = ctx.enter_context(tc.psum_pool(name="psum", bufs=PSUM_BANKS))
 
         x_sb, x_grouped, x_codes, x_scales = {}, {}, {}, {}
         d_grouped, d_codes, d_scales = {}, {}, {}
@@ -109,7 +107,7 @@ def tile_multiheadlatentattention_pb_t_kernel(
             x_grouped[c] = grouped_pool.tile([P, CHUNK_TOKENS * PACK], BF16, name="x_grouped", align_bytes=64)
             grouped_words = x_grouped[c][:].bitcast(F32).rearrange("p (j w u) -> p j w u", j=CHUNK, u=2)
             for pair in range(CHUNK // 2):
-                x_t = psum_xt.tile([P, 2, 2, P], F32, name="x_t")
+                x_t = psum.tile([P, 2, 2, P], F32, name="x_t", tag="bank")
                 for j in range(2):
                     words = x_sb[c][:, 2 * pair + j, :].bitcast(F32)
                     for u in range(2):
@@ -129,7 +127,7 @@ def tile_multiheadlatentattention_pb_t_kernel(
             if j == 0:
                 d_grouped[c] = grouped_pool.tile([P, CHUNK, P, PACK], BF16, name="d_grouped", align_bytes=64)
             tokens = slice(j * P, (j + 1) * P)
-            down_t = psum_down.tile([P, PACK, P], F32, name="down_t")
+            down_t = psum.tile([P, PACK, P], F32, name="down_t", tag="bank")
             for f in range(PACK):
                 cols = slice(f * P, (f + 1) * P)
                 nc.tensor.matmul_mx(
@@ -155,7 +153,7 @@ def tile_multiheadlatentattention_pb_t_kernel(
                 return
             first = place(c)[1]
             k_sb[c] = keys_pool.tile([P, HEADS, CHUNK, D_KEY], F32, name="k_sb")
-            k_r = psum_rope.tile([P, CHUNK, ROPE_COLS], F32, name="k_r")
+            k_r = psum.tile([P, CHUNK, ROPE_COLS], F32, name="k_r", tag="bank")
             for j in range(CHUNK):
                 tokens = slice(j * P, (j + 1) * P)
                 nc.tensor.matmul_mx(
@@ -184,7 +182,7 @@ def tile_multiheadlatentattention_pb_t_kernel(
                     in1=table[:, positions, :].unsqueeze(2).to_broadcast([P, CHUNK, HEADS, PAIRS]),
                     op=MULT,
                 )
-            nc.vector.tensor_tensor(
+            nc.gpsimd.tensor_tensor(
                 out=k_sb[c][:, :, :, D_HEAD:D_KEY].rearrange("p h j (i e) -> p h j i e", e=2),
                 in0=by_cos[:].rearrange("p h j (i e) -> p h j i e", e=2),
                 in1=by_sin[:].rearrange("p e h j i -> p h j i e"),
@@ -197,7 +195,7 @@ def tile_multiheadlatentattention_pb_t_kernel(
             if j == 0:
                 v_sb[c] = values_pool.tile([P, HEADS, CHUNK, D_HEAD], F32, name="v_sb")
             tokens = slice(j * P, (j + 1) * P)
-            kc_v = psum_up.tile([P, 2, HEADS, D_HEAD], F32, name="kc_v")
+            kc_v = psum.tile([P, 2, HEADS, D_HEAD], F32, name="kc_v", tag="bank")
             nc.tensor.matmul_mx(
                 out=kc_v[:].rearrange("p s h f -> p (s h f)"),
                 lhsT=d_codes[c][:, tokens].bitcast(FP8X4),

@@ -53,7 +53,7 @@ def tile_multiheadlatentattention_pb_t_kernel(
 
         x_sb, x_grouped, x_codes, x_scales = {}, {}, {}, {}
         d_grouped, d_codes, d_scales = {}, {}, {}
-        k_sb, v_sb = {}, {}
+        k_r_banks, k_sb, v_sb = {}, {}, {}
 
         def live(c):
             return 0 <= c < N_CHUNKS
@@ -148,12 +148,11 @@ def tile_multiheadlatentattention_pb_t_kernel(
                 "d", d_grouped[c][:].rearrange("p j w f -> p (j w f)"), CHUNK_TOKENS, codes_pool
             )
 
-        def rope(c):
+        def rope_products(c):
             if not live(c):
                 return
-            first = place(c)[1]
-            k_sb[c] = keys_pool.tile([P, HEADS, CHUNK, D_KEY], F32, name="k_sb")
             k_r = psum.tile([P, CHUNK, ROPE_COLS], F32, name="k_r", tag="bank")
+            k_r_banks[c] = k_r
             for j in range(CHUNK):
                 tokens = slice(j * P, (j + 1) * P)
                 nc.tensor.matmul_mx(
@@ -165,7 +164,14 @@ def tile_multiheadlatentattention_pb_t_kernel(
                     start=True,
                     stop=True,
                 )
+
+        def rotate(c):
+            if not live(c):
+                return
+            first = place(c)[1]
             positions = slice(first, first + CHUNK)
+            k_r = k_r_banks[c]
+            k_sb[c] = keys_pool.tile([P, HEADS, CHUNK, D_KEY], F32, name="k_sb")
             by_cos = rope_pool.tile([P, HEADS, CHUNK, D_ROPE], F32, name="by_cos")
             nc.vector.tensor_tensor(
                 out=by_cos[:].rearrange("p h j f -> p j h f"),
@@ -232,16 +238,17 @@ def tile_multiheadlatentattention_pb_t_kernel(
         def step(s):
             quantise_x(s + 2)
             quantise_down(s)
+            rotate(s + 1)
             down(s + 1, 0)
             up(s - 1, 0)
             down(s + 1, 1)
             up(s - 1, 1)
-            rope(s + 1)
             down(s + 1, 2)
             up(s - 1, 2)
             transpose_chunk(s + 3)
             down(s + 1, 3)
             up(s - 1, 3)
+            rope_products(s + 2)
             store(s - 1)
 
         wd_grouped = consts.tile([P, PACK, P, PACK], BF16, align_bytes=64)
@@ -250,8 +257,8 @@ def tile_multiheadlatentattention_pb_t_kernel(
         wr_grouped = consts.tile([P, ROPE_COLS, PACK], BF16, align_bytes=64)
         nc.scalar.copy(out=wr_grouped[:], in_=wr_raw[:].rearrange("p t n -> p n t"))
         step(-3)
-        step(-2)
         wr_codes, wr_scales = quantise("wr", wr_grouped[:].rearrange("p n t -> p (n t)"), ROPE_COLS, consts)
+        step(-2)
         cos_twice = consts.tile([P, POSITIONS, D_ROPE], BF16)
         sin_minus = consts.tile([P, POSITIONS, PAIRS], BF16)
         rope_tables(0)

@@ -58,9 +58,6 @@ def tile_multiheadlatentattention_pb_t_kernel(
         def live(c):
             return 0 <= c < N_CHUNKS
 
-        def copy_out(piece):
-            return nc.scalar.copy if piece % 2 == 0 else nc.vector.tensor_copy
-
         def place(c):
             return c // CHUNKS_PER_SEQ, (c % CHUNKS_PER_SEQ) * CHUNK
 
@@ -112,7 +109,7 @@ def tile_multiheadlatentattention_pb_t_kernel(
                     words = x_sb[c][:, 2 * pair + j, :].bitcast(F32)
                     for u in range(2):
                         nc.tensor.transpose(x_t[:, j, u, :], words[:, u * P : (u + 1) * P], ident[:])
-                copy_out(pair)(
+                nc.scalar.copy(
                     out=grouped_words[:, 2 * pair : 2 * pair + 2], in_=x_t[:].rearrange("p j u w -> p j w u")
                 )
 
@@ -139,7 +136,8 @@ def tile_multiheadlatentattention_pb_t_kernel(
                     start=True,
                     stop=True,
                 )
-            nc.scalar.copy(out=d_grouped[c][:, j], in_=down_t[:].rearrange("p f w -> p w f"))
+            copy = nc.scalar.copy if j == CHUNK - 1 else nc.vector.tensor_copy
+            copy(out=d_grouped[c][:, j], in_=down_t[:].rearrange("p f w -> p w f"))
 
         def quantise_down(c):
             if not live(c):
@@ -195,24 +193,29 @@ def tile_multiheadlatentattention_pb_t_kernel(
                 op=ADD,
             )
 
-        def up(c, j):
+        def up(c, pair):
             if not live(c):
                 return
-            if j == 0:
+            if pair == 0:
                 v_sb[c] = values_pool.tile([P, HEADS, CHUNK, D_HEAD], F32, name="v_sb")
-            tokens = slice(j * P, (j + 1) * P)
-            kc_v = psum.tile([P, 2, HEADS, D_HEAD], F32, name="kc_v", tag="bank")
-            nc.tensor.matmul_mx(
-                out=kc_v[:].rearrange("p s h f -> p (s h f)"),
-                lhsT=d_codes[c][:, tokens].bitcast(FP8X4),
-                lhsT_scale=d_scales[c][:, tokens],
-                rhs=wup_codes[:].bitcast(FP8X4),
-                rhs_scale=wup_scales[:],
-                start=True,
-                stop=True,
-            )
-            copy_out(j)(out=k_sb[c][:, :, j, 0:D_HEAD], in_=kc_v[:, 0])
-            copy_out(j)(out=v_sb[c][:, :, j, :], in_=kc_v[:, 1])
+            k_c = psum.tile([P, 2, HEADS, D_HEAD], F32, name="k_c", tag="bank")
+            v = psum.tile([P, 2, HEADS, D_HEAD], F32, name="v", tag="bank")
+            for j in range(2):
+                tokens = slice((2 * pair + j) * P, (2 * pair + j + 1) * P)
+                for bank, cols in ((k_c, slice(0, UP_COLS // 2)), (v, slice(UP_COLS // 2, UP_COLS))):
+                    nc.tensor.matmul_mx(
+                        out=bank[:, j].rearrange("p h f -> p (h f)"),
+                        lhsT=d_codes[c][:, tokens].bitcast(FP8X4),
+                        lhsT_scale=d_scales[c][:, tokens],
+                        rhs=wup_codes[:, cols].bitcast(FP8X4),
+                        rhs_scale=wup_scales[:, cols],
+                        start=True,
+                        stop=True,
+                    )
+            tiles = slice(2 * pair, 2 * pair + 2)
+            nc.scalar.copy(out=k_sb[c][:, :, tiles, 0:D_HEAD], in_=k_c[:].rearrange("p j h f -> p h j f"))
+            copy_v = nc.vector.tensor_copy if c == N_CHUNKS - 1 else nc.scalar.copy
+            copy_v(out=v_sb[c][:, :, tiles, :], in_=v[:].rearrange("p j h f -> p h j f"))
 
         def store(c):
             if not live(c):
@@ -242,12 +245,10 @@ def tile_multiheadlatentattention_pb_t_kernel(
             down(s + 1, 0)
             up(s - 1, 0)
             down(s + 1, 1)
-            up(s - 1, 1)
-            down(s + 1, 2)
-            up(s - 1, 2)
             transpose_chunk(s + 3)
+            down(s + 1, 2)
+            up(s - 1, 1)
             down(s + 1, 3)
-            up(s - 1, 3)
             rope_products(s + 2)
             store(s - 1)
 

@@ -58,6 +58,9 @@ def tile_multiheadlatentattention_pb_t_kernel(
         def live(c):
             return 0 <= c < N_CHUNKS
 
+        def copy_out(piece):
+            return nc.scalar.copy if piece % 2 == 0 else nc.vector.tensor_copy
+
         def place(c):
             return c // CHUNKS_PER_SEQ, (c % CHUNKS_PER_SEQ) * CHUNK
 
@@ -109,7 +112,7 @@ def tile_multiheadlatentattention_pb_t_kernel(
                     words = x_sb[c][:, 2 * pair + j, :].bitcast(F32)
                     for u in range(2):
                         nc.tensor.transpose(x_t[:, j, u, :], words[:, u * P : (u + 1) * P], ident[:])
-                nc.scalar.copy(
+                copy_out(pair)(
                     out=grouped_words[:, 2 * pair : 2 * pair + 2], in_=x_t[:].rearrange("p j u w -> p j w u")
                 )
 
@@ -136,8 +139,7 @@ def tile_multiheadlatentattention_pb_t_kernel(
                     start=True,
                     stop=True,
                 )
-            copy = nc.scalar.copy if j == CHUNK - 1 else nc.vector.tensor_copy
-            copy(out=d_grouped[c][:, j], in_=down_t[:].rearrange("p f w -> p w f"))
+            nc.scalar.copy(out=d_grouped[c][:, j], in_=down_t[:].rearrange("p f w -> p w f"))
 
         def quantise_down(c):
             if not live(c):
@@ -193,49 +195,45 @@ def tile_multiheadlatentattention_pb_t_kernel(
                 op=ADD,
             )
 
-        def up(c, pair):
+        def up(c, j):
             if not live(c):
                 return
-            if pair == 0:
+            if j == 0:
                 v_sb[c] = values_pool.tile([P, HEADS, CHUNK, D_HEAD], F32, name="v_sb")
-            k_c = psum.tile([P, 2, HEADS, D_HEAD], F32, name="k_c", tag="bank")
-            v = psum.tile([P, 2, HEADS, D_HEAD], F32, name="v", tag="bank")
-            for j in range(2):
-                tokens = slice((2 * pair + j) * P, (2 * pair + j + 1) * P)
-                for bank, cols in ((k_c, slice(0, UP_COLS // 2)), (v, slice(UP_COLS // 2, UP_COLS))):
-                    nc.tensor.matmul_mx(
-                        out=bank[:, j].rearrange("p h f -> p (h f)"),
-                        lhsT=d_codes[c][:, tokens].bitcast(FP8X4),
-                        lhsT_scale=d_scales[c][:, tokens],
-                        rhs=wup_codes[:, cols].bitcast(FP8X4),
-                        rhs_scale=wup_scales[:, cols],
-                        start=True,
-                        stop=True,
-                    )
-            tiles = slice(2 * pair, 2 * pair + 2)
-            nc.scalar.copy(out=k_sb[c][:, :, tiles, 0:D_HEAD], in_=k_c[:].rearrange("p j h f -> p h j f"))
-            copy_v = nc.vector.tensor_copy if c == N_CHUNKS - 1 else nc.scalar.copy
-            copy_v(out=v_sb[c][:, :, tiles, :], in_=v[:].rearrange("p j h f -> p h j f"))
+            tokens = slice(j * P, (j + 1) * P)
+            kc_v = psum.tile([P, 2, HEADS, D_HEAD], F32, name="kc_v", tag="bank")
+            nc.tensor.matmul_mx(
+                out=kc_v[:].rearrange("p s h f -> p (s h f)"),
+                lhsT=d_codes[c][:, tokens].bitcast(FP8X4),
+                lhsT_scale=d_scales[c][:, tokens],
+                rhs=wup_codes[:].bitcast(FP8X4),
+                rhs_scale=wup_scales[:],
+                start=True,
+                stop=True,
+            )
+            copy_out(j)(out=k_sb[c][:, :, j, 0:D_HEAD], in_=kc_v[:, 0])
+            copy_out(j)(out=v_sb[c][:, :, j, :], in_=kc_v[:, 1])
 
-        def store(c):
+        def store(c, half):
             if not live(c):
                 return
             b, first = place(c)
-            nc.sync.dma_start(out=keys_view[b, :, :, first : first + CHUNK, :], in_=k_sb[c][:])
-            nc.sync.dma_start(out=values_view[b, :, :, first : first + CHUNK, :], in_=v_sb[c][:])
+            if c == N_CHUNKS - 1:
+                lo, hi = half * CHUNK // 2, (half + 1) * CHUNK // 2
+            elif half == 1:
+                lo, hi = 0, CHUNK
+            else:
+                return
+            nc.sync.dma_start(out=keys_view[b, :, :, first + lo : first + hi, :], in_=k_sb[c][:, :, lo:hi, :])
+            nc.sync.dma_start(out=values_view[b, :, :, first + lo : first + hi, :], in_=v_sb[c][:, :, lo:hi, :])
 
-        def rope_tables(g):
+        def cos_table(g):
+            if not 0 <= g < CHUNKS_PER_SEQ:
+                return
             positions = slice(g * CHUNK, (g + 1) * CHUNK)
-            nc.gpsimd.tensor_scalar(
+            nc.scalar.copy(
                 out=cos_twice[:, positions, :].rearrange("p t (i e) -> p t i e", e=2),
-                in0=cos_raw[:, positions, :].unsqueeze(3).to_broadcast([P, CHUNK, PAIRS, 2]),
-                scalar1=1.0,
-                scalar2=0.0,
-                op0=MULT,
-                op1=ADD,
-            )
-            nc.gpsimd.tensor_scalar(
-                out=sin_minus[:, positions, :], in0=sin_raw[:, positions, :], scalar1=-1.0, scalar2=0.0, op0=MULT, op1=ADD
+                in_=cos_raw[:, positions, :].unsqueeze(3).to_broadcast([P, CHUNK, PAIRS, 2]),
             )
 
         def step(s):
@@ -245,31 +243,38 @@ def tile_multiheadlatentattention_pb_t_kernel(
             down(s + 1, 0)
             up(s - 1, 0)
             down(s + 1, 1)
-            transpose_chunk(s + 3)
-            down(s + 1, 2)
             up(s - 1, 1)
+            store(s - 1, 0)
+            down(s + 1, 2)
+            up(s - 1, 2)
+            transpose_chunk(s + 3)
             down(s + 1, 3)
+            up(s - 1, 3)
             rope_products(s + 2)
-            store(s - 1)
+            cos_table(s + 2)
+            store(s - 1, 1)
 
         wd_grouped = consts.tile([P, PACK, P, PACK], BF16, align_bytes=64)
         nc.vector.tensor_copy(out=wd_grouped[:], in_=wd_raw[:].rearrange("p t (m f) -> p f m t", f=PACK))
         wd_codes, wd_scales = quantise("wd", wd_grouped[:].rearrange("p f m t -> p (f m t)"), D_LATENT, consts)
         wr_grouped = consts.tile([P, ROPE_COLS, PACK], BF16, align_bytes=64)
         nc.scalar.copy(out=wr_grouped[:], in_=wr_raw[:].rearrange("p t n -> p n t"))
+        cos_twice = consts.tile([P, POSITIONS, D_ROPE], BF16)
         step(-3)
         wr_codes, wr_scales = quantise("wr", wr_grouped[:].rearrange("p n t -> p (n t)"), ROPE_COLS, consts)
         step(-2)
-        cos_twice = consts.tile([P, POSITIONS, D_ROPE], BF16)
         sin_minus = consts.tile([P, POSITIONS, PAIRS], BF16)
-        rope_tables(0)
-        rope_tables(1)
+        nc.vector.tensor_scalar(out=sin_minus[:], in0=sin_raw[:], scalar1=-1.0, scalar2=None, op0=MULT)
         wup_grouped = consts.tile([P, UP_COLS, PACK], BF16, align_bytes=64)
-        nc.gpsimd.tensor_scalar(
-            out=wup_grouped[:], in0=wup_raw[:].rearrange("p t n -> p n t"), scalar1=1.0, scalar2=0.0, op0=MULT, op1=ADD
-        )
-        for g in range(2, CHUNKS_PER_SEQ):
-            rope_tables(g)
+        for cols in (slice(n, n + P) for n in range(0, UP_COLS, P)):
+            nc.gpsimd.tensor_scalar(
+                out=wup_grouped[:, cols, :],
+                in0=wup_raw[:, :, cols].rearrange("p t n -> p n t"),
+                scalar1=1.0,
+                scalar2=0.0,
+                op0=MULT,
+                op1=ADD,
+            )
         step(-1)
         step(0)
         wup_codes, wup_scales = quantise("wup", wup_grouped[:].rearrange("p n t -> p (n t)"), UP_COLS, consts)

@@ -195,24 +195,28 @@ def tile_multiheadlatentattention_pb_t_kernel(
                 op=ADD,
             )
 
-        def up(c, j):
+        def up(c, pair):
             if not live(c):
                 return
-            if j == 0:
+            if pair == 0:
                 v_sb[c] = values_pool.tile([P, HEADS, CHUNK, D_HEAD], F32, name="v_sb")
-            tokens = slice(j * P, (j + 1) * P)
-            kc_v = psum.tile([P, 2, HEADS, D_HEAD], F32, name="kc_v", tag="bank")
-            nc.tensor.matmul_mx(
-                out=kc_v[:].rearrange("p s h f -> p (s h f)"),
-                lhsT=d_codes[c][:, tokens].bitcast(FP8X4),
-                lhsT_scale=d_scales[c][:, tokens],
-                rhs=wup_codes[:].bitcast(FP8X4),
-                rhs_scale=wup_scales[:],
-                start=True,
-                stop=True,
-            )
-            copy_out(j)(out=k_sb[c][:, :, j, 0:D_HEAD], in_=kc_v[:, 0])
-            copy_out(j)(out=v_sb[c][:, :, j, :], in_=kc_v[:, 1])
+            k_c = psum.tile([P, 2, HEADS, D_HEAD], F32, name="k_c", tag="bank")
+            v = psum.tile([P, 2, HEADS, D_HEAD], F32, name="v", tag="bank")
+            for j in range(2):
+                tokens = slice((2 * pair + j) * P, (2 * pair + j + 1) * P)
+                for bank, cols in ((k_c, slice(0, UP_COLS // 2)), (v, slice(UP_COLS // 2, UP_COLS))):
+                    nc.tensor.matmul_mx(
+                        out=bank[:, j].rearrange("p h f -> p (h f)"),
+                        lhsT=d_codes[c][:, tokens].bitcast(FP8X4),
+                        lhsT_scale=d_scales[c][:, tokens],
+                        rhs=wup_codes[:, cols].bitcast(FP8X4),
+                        rhs_scale=wup_scales[:, cols],
+                        start=True,
+                        stop=True,
+                    )
+            tiles = slice(2 * pair, 2 * pair + 2)
+            nc.scalar.copy(out=k_sb[c][:, :, tiles, 0:D_HEAD], in_=k_c[:].rearrange("p j h f -> p h j f"))
+            nc.vector.tensor_copy(out=v_sb[c][:, :, tiles, :], in_=v[:].rearrange("p j h f -> p h j f"))
 
         def store(c, half):
             if not live(c):
@@ -242,14 +246,12 @@ def tile_multiheadlatentattention_pb_t_kernel(
             rotate(s + 1)
             down(s + 1, 0)
             up(s - 1, 0)
-            down(s + 1, 1)
-            up(s - 1, 1)
             store(s - 1, 0)
+            down(s + 1, 1)
             down(s + 1, 2)
-            up(s - 1, 2)
             transpose_chunk(s + 3)
             down(s + 1, 3)
-            up(s - 1, 3)
+            up(s - 1, 1)
             rope_products(s + 2)
             cos_table(s + 2)
             store(s - 1, 1)

@@ -47,9 +47,10 @@ def tile_multiheadlatentattention_pb_t_kernel(
         grouped_pool = ctx.enter_context(tc.tile_pool(name="grouped_pool", bufs=2))
         codes_pool = ctx.enter_context(tc.tile_pool(name="codes_pool", bufs=3))
         rope_pool = ctx.enter_context(tc.tile_pool(name="rope_pool", bufs=2))
-        keys_pool = ctx.enter_context(tc.tile_pool(name="keys_pool", bufs=5))
+        keys_pool = ctx.enter_context(tc.tile_pool(name="keys_pool", bufs=4))
         values_pool = ctx.enter_context(tc.tile_pool(name="values_pool", bufs=3))
-        psum = ctx.enter_context(tc.psum_pool(name="psum", bufs=PSUM_BANKS))
+        psum_k_r = ctx.enter_context(tc.psum_pool(name="psum_k_r", bufs=1))
+        psum = ctx.enter_context(tc.psum_pool(name="psum", bufs=PSUM_BANKS - 1))
 
         x_sb, x_grouped, x_codes, x_scales = {}, {}, {}, {}
         d_grouped, d_codes, d_scales = {}, {}, {}
@@ -91,11 +92,10 @@ def tile_multiheadlatentattention_pb_t_kernel(
         nc.sync.dma_start(out=cos_raw[:], in_=rope_cos.rearrange("(p t) i -> p t i", t=POSITIONS))
         sin_raw = consts.tile([P, POSITIONS, PAIRS], BF16)
         nc.sync.dma_start(out=sin_raw[:], in_=rope_sin.rearrange("(p t) i -> p t i", t=POSITIONS))
-        load_chunk(2)
         wup_raw = consts.tile([P, PACK, UP_COLS], BF16)
         nc.sync.dma_start(out=wup_raw[:, :, 0 : UP_COLS // 2], in_=W_k_up.rearrange("(p t) n -> p t n", t=PACK))
         nc.sync.dma_start(out=wup_raw[:, :, UP_COLS // 2 : UP_COLS], in_=W_v_up.rearrange("(p t) n -> p t n", t=PACK))
-        for c in range(3, N_CHUNKS):
+        for c in range(2, N_CHUNKS):
             load_chunk(c)
 
         ident = consts.tile([P, P], F32)
@@ -151,7 +151,7 @@ def tile_multiheadlatentattention_pb_t_kernel(
         def rope_products(c):
             if not live(c):
                 return
-            k_r = psum.tile([P, CHUNK, ROPE_COLS], F32, name="k_r", tag="bank")
+            k_r = psum_k_r.tile([P, CHUNK, ROPE_COLS], F32, name="k_r")
             k_r_banks[c] = k_r
             for j in range(CHUNK):
                 tokens = slice(j * P, (j + 1) * P)
@@ -195,28 +195,24 @@ def tile_multiheadlatentattention_pb_t_kernel(
                 op=ADD,
             )
 
-        def up(c, pair):
+        def up(c, j):
             if not live(c):
                 return
-            if pair == 0:
+            if j == 0:
                 v_sb[c] = values_pool.tile([P, HEADS, CHUNK, D_HEAD], F32, name="v_sb")
-            k_c = psum.tile([P, 2, HEADS, D_HEAD], F32, name="k_c", tag="bank")
-            v = psum.tile([P, 2, HEADS, D_HEAD], F32, name="v", tag="bank")
-            for j in range(2):
-                tokens = slice((2 * pair + j) * P, (2 * pair + j + 1) * P)
-                for bank, cols in ((k_c, slice(0, UP_COLS // 2)), (v, slice(UP_COLS // 2, UP_COLS))):
-                    nc.tensor.matmul_mx(
-                        out=bank[:, j].rearrange("p h f -> p (h f)"),
-                        lhsT=d_codes[c][:, tokens].bitcast(FP8X4),
-                        lhsT_scale=d_scales[c][:, tokens],
-                        rhs=wup_codes[:, cols].bitcast(FP8X4),
-                        rhs_scale=wup_scales[:, cols],
-                        start=True,
-                        stop=True,
-                    )
-            tiles = slice(2 * pair, 2 * pair + 2)
-            nc.scalar.copy(out=k_sb[c][:, :, tiles, 0:D_HEAD], in_=k_c[:].rearrange("p j h f -> p h j f"))
-            nc.vector.tensor_copy(out=v_sb[c][:, :, tiles, :], in_=v[:].rearrange("p j h f -> p h j f"))
+            tokens = slice(j * P, (j + 1) * P)
+            kc_v = psum.tile([P, 2, HEADS, D_HEAD], F32, name="kc_v", tag="bank")
+            nc.tensor.matmul_mx(
+                out=kc_v[:].rearrange("p s h f -> p (s h f)"),
+                lhsT=d_codes[c][:, tokens].bitcast(FP8X4),
+                lhsT_scale=d_scales[c][:, tokens],
+                rhs=wup_codes[:].bitcast(FP8X4),
+                rhs_scale=wup_scales[:],
+                start=True,
+                stop=True,
+            )
+            copy_out(j)(out=k_sb[c][:, :, j, 0:D_HEAD], in_=kc_v[:, 0])
+            copy_out(j)(out=v_sb[c][:, :, j, :], in_=kc_v[:, 1])
 
         def store(c, half):
             if not live(c):
@@ -241,20 +237,20 @@ def tile_multiheadlatentattention_pb_t_kernel(
             )
 
         def step(s):
-            quantise_x(s + 2)
             quantise_down(s)
+            quantise_x(s + 2)
             rotate(s + 1)
-            down(s + 1, 0)
-            up(s - 1, 0)
-            store(s - 1, 0)
-            down(s + 1, 1)
-            down(s + 1, 2)
+            for j in range(CHUNK):
+                down(s + 1, j)
             transpose_chunk(s + 3)
-            down(s + 1, 3)
-            up(s - 1, 1)
+            up(s, 0)
+            up(s, 1)
+            store(s, 0)
+            up(s, 2)
+            up(s, 3)
             rope_products(s + 2)
             cos_table(s + 2)
-            store(s - 1, 1)
+            store(s, 1)
 
         wd_grouped = consts.tile([P, PACK, P, PACK], BF16, align_bytes=64)
         nc.vector.tensor_copy(out=wd_grouped[:], in_=wd_raw[:].rearrange("p t (m f) -> p f m t", f=PACK))
@@ -278,7 +274,6 @@ def tile_multiheadlatentattention_pb_t_kernel(
                 op1=ADD,
             )
         step(-1)
-        step(0)
         wup_codes, wup_scales = quantise("wup", wup_grouped[:].rearrange("p n t -> p (n t)"), UP_COLS, consts)
-        for s in range(1, N_CHUNKS + 1):
+        for s in range(N_CHUNKS):
             step(s)

@@ -47,8 +47,8 @@ def tile_multiheadlatentattention_pb_t_kernel(
         grouped_pool = ctx.enter_context(tc.tile_pool(name="grouped_pool", bufs=2))
         codes_pool = ctx.enter_context(tc.tile_pool(name="codes_pool", bufs=3))
         rope_pool = ctx.enter_context(tc.tile_pool(name="rope_pool", bufs=2))
-        keys_pool = ctx.enter_context(tc.tile_pool(name="keys_pool", bufs=4))
-        values_pool = ctx.enter_context(tc.tile_pool(name="values_pool", bufs=3))
+        keys_pool = ctx.enter_context(tc.tile_pool(name="keys_pool", bufs=8))
+        values_pool = ctx.enter_context(tc.tile_pool(name="values_pool", bufs=8))
         psum_k_r = ctx.enter_context(tc.psum_pool(name="psum_k_r", bufs=1))
         psum = ctx.enter_context(tc.psum_pool(name="psum", bufs=PSUM_BANKS - 1))
 

@@ -49,12 +49,13 @@ def tile_multiheadlatentattention_pb_t_kernel(
         rope_pool = ctx.enter_context(tc.tile_pool(name="rope_pool", bufs=2))
         keys_pool = ctx.enter_context(tc.tile_pool(name="keys_pool", bufs=8))
         values_pool = ctx.enter_context(tc.tile_pool(name="values_pool", bufs=8))
-        psum_k_r = ctx.enter_context(tc.psum_pool(name="psum_k_r", bufs=1))
-        psum = ctx.enter_context(tc.psum_pool(name="psum", bufs=PSUM_BANKS - 1))
+        psum_k_r = ctx.enter_context(tc.psum_pool(name="psum_k_r", bufs=2))
+        psum = ctx.enter_context(tc.psum_pool(name="psum", bufs=PSUM_BANKS - 2))
 
         x_sb, x_grouped, x_codes, x_scales = {}, {}, {}, {}
         d_grouped, d_codes, d_scales = {}, {}, {}
         k_r_banks, k_sb, v_sb = {}, {}, {}
+        by_cos_tiles = {}
 
         def live(c):
             return 0 <= c < N_CHUNKS
@@ -165,33 +166,39 @@ def tile_multiheadlatentattention_pb_t_kernel(
                     stop=True,
                 )
 
-        def rotate(c):
+        def rotate_cos(c):
             if not live(c):
                 return
             first = place(c)[1]
             positions = slice(first, first + CHUNK)
             k_r = k_r_banks[c]
             k_sb[c] = keys_pool.tile([P, HEADS, CHUNK, D_KEY], F32, name="k_sb")
-            by_cos = rope_pool.tile([P, HEADS, CHUNK, D_ROPE], F32, name="by_cos")
+            by_cos = rope_pool.tile([P, CHUNK, 2 * HEADS, PAIRS], F32, name="by_cos")
+            by_cos_tiles[c] = by_cos
             nc.vector.tensor_tensor(
-                out=by_cos[:].rearrange("p h j f -> p j h f"),
-                in0=k_r[:].rearrange("p j (h f) -> p j h f", h=HEADS),
-                in1=cos_twice[:, positions, :].unsqueeze(2).to_broadcast([P, CHUNK, HEADS, D_ROPE]),
+                out=by_cos[:],
+                in0=k_r[:].rearrange("p j (g i) -> p j g i", i=PAIRS),
+                in1=cos_raw[:, positions, :].unsqueeze(2).to_broadcast([P, CHUNK, 2 * HEADS, PAIRS]),
                 op=MULT,
             )
-            by_sin = rope_pool.tile([P, 2, HEADS, CHUNK, PAIRS], F32, name="by_sin")
-            k_r_pairs = k_r[:].rearrange("p j (h i e) -> p j h i e", h=HEADS, e=2)
-            for e, table in ((0, sin_minus), (1, sin_raw)):
-                nc.vector.tensor_tensor(
-                    out=by_sin[:, e].rearrange("p h j i -> p j h i"),
-                    in0=k_r_pairs[:, :, :, :, 1 - e],
-                    in1=table[:, positions, :].unsqueeze(2).to_broadcast([P, CHUNK, HEADS, PAIRS]),
-                    op=MULT,
-                )
+        def rotate_sin(c):
+            if not live(c):
+                return
+            first = place(c)[1]
+            positions = slice(first, first + CHUNK)
+            k_r = k_r_banks[c]
+            by_cos = by_cos_tiles[c]
+            by_sin = rope_pool.tile([P, CHUNK, HEADS, 2, PAIRS], F32, name="by_sin")
+            nc.vector.tensor_tensor(
+                out=by_sin[:],
+                in0=k_r[:].rearrange("p j (h e i) -> p j h e i", h=HEADS, e=2)[:, :, :, ::-1, :],
+                in1=sin_signed[:, positions].unsqueeze(2).to_broadcast([P, CHUNK, HEADS, 2, PAIRS]),
+                op=MULT,
+            )
             nc.gpsimd.tensor_tensor(
-                out=k_sb[c][:, :, :, D_HEAD:D_KEY].rearrange("p h j (i e) -> p h j i e", e=2),
-                in0=by_cos[:].rearrange("p h j (i e) -> p h j i e", e=2),
-                in1=by_sin[:].rearrange("p e h j i -> p h j i e"),
+                out=k_sb[c][:, :, :, D_HEAD:D_KEY].rearrange("p h j (i e) -> p j h i e", e=2),
+                in0=by_cos[:].rearrange("p j (h e) i -> p j h i e", e=2),
+                in1=by_sin[:].rearrange("p j h e i -> p j h i e"),
                 op=ADD,
             )
 
@@ -227,19 +234,11 @@ def tile_multiheadlatentattention_pb_t_kernel(
             nc.sync.dma_start(out=keys_view[b, :, :, first + lo : first + hi, :], in_=k_sb[c][:, :, lo:hi, :])
             nc.sync.dma_start(out=values_view[b, :, :, first + lo : first + hi, :], in_=v_sb[c][:, :, lo:hi, :])
 
-        def cos_table(g):
-            if not 0 <= g < CHUNKS_PER_SEQ:
-                return
-            positions = slice(g * CHUNK, (g + 1) * CHUNK)
-            nc.scalar.copy(
-                out=cos_twice[:, positions, :].rearrange("p t (i e) -> p t i e", e=2),
-                in_=cos_raw[:, positions, :].unsqueeze(3).to_broadcast([P, CHUNK, PAIRS, 2]),
-            )
-
         def step(s):
             quantise_down(s)
             quantise_x(s + 2)
-            rotate(s + 1)
+            rotate_sin(s)
+            rotate_cos(s + 1)
             for j in range(CHUNK):
                 down(s + 1, j)
             transpose_chunk(s + 3)
@@ -249,20 +248,24 @@ def tile_multiheadlatentattention_pb_t_kernel(
             up(s, 2)
             up(s, 3)
             rope_products(s + 2)
-            cos_table(s + 2)
             store(s, 1)
 
         wd_grouped = consts.tile([P, PACK, P, PACK], BF16, align_bytes=64)
         nc.vector.tensor_copy(out=wd_grouped[:], in_=wd_raw[:].rearrange("p t (m f) -> p f m t", f=PACK))
         wd_codes, wd_scales = quantise("wd", wd_grouped[:].rearrange("p f m t -> p (f m t)"), D_LATENT, consts)
         wr_grouped = consts.tile([P, ROPE_COLS, PACK], BF16, align_bytes=64)
-        nc.scalar.copy(out=wr_grouped[:], in_=wr_raw[:].rearrange("p t n -> p n t"))
-        cos_twice = consts.tile([P, POSITIONS, D_ROPE], BF16)
+        for h in range(HEADS):
+            cols = slice(h * D_ROPE, (h + 1) * D_ROPE)
+            nc.scalar.copy(
+                out=wr_grouped[:, cols, :].rearrange("p (e i) t -> p e i t", e=2),
+                in_=wr_raw[:, :, cols].rearrange("p t (i e) -> p e i t", e=2),
+            )
         step(-3)
         wr_codes, wr_scales = quantise("wr", wr_grouped[:].rearrange("p n t -> p (n t)"), ROPE_COLS, consts)
         step(-2)
-        sin_minus = consts.tile([P, POSITIONS, PAIRS], BF16)
-        nc.vector.tensor_scalar(out=sin_minus[:], in0=sin_raw[:], scalar1=-1.0, scalar2=None, op0=MULT)
+        sin_signed = consts.tile([P, POSITIONS, 2, PAIRS], BF16)
+        nc.vector.tensor_scalar(out=sin_signed[:, :, 0, :], in0=sin_raw[:], scalar1=-1.0, scalar2=None, op0=MULT)
+        nc.vector.tensor_copy(out=sin_signed[:, :, 1, :], in_=sin_raw[:])
         wup_grouped = consts.tile([P, UP_COLS, PACK], BF16, align_bytes=64)
         for cols in (slice(n, n + P) for n in range(0, UP_COLS, P)):
             nc.gpsimd.tensor_scalar(

@@ -23,6 +23,7 @@ CHUNK = 4
 CHUNK_TOKENS = CHUNK * P
 CHUNKS_PER_SEQ = POSITIONS // CHUNK
 N_CHUNKS = BATCH * CHUNKS_PER_SEQ
+RUN = 4
 UP_COLS = 2 * HEADS * D_HEAD
 ROPE_COLS = HEADS * D_ROPE
 
@@ -140,7 +141,10 @@ def tile_multiheadlatentattention_pb_t_kernel(
                     start=True,
                     stop=True,
                 )
-            nc.scalar.copy(out=d_grouped[c][:, j], in_=down_t[:].rearrange("p f w -> p w f"))
+            nc.scalar.copy(
+                out=d_grouped[c][:, j].rearrange("p (g i) f -> p g f i", i=RUN),
+                in_=down_t[:].rearrange("p f (g i) -> p g f i", i=RUN),
+            )
 
         def quantise_down(c):
             if not live(c):

@@ -90,14 +90,16 @@ def tile_multiheadlatentattention_pb_t_kernel(
             in_=W_k_rope.rearrange("(u p e) n -> p u e n", u=2, e=2),
         )
         load_chunk(1)
+        wk_raw = consts.tile([P, PACK, UP_COLS // 2], BF16)
+        nc.sync.dma_start(out=wk_raw[:], in_=W_k_up.rearrange("(p t) n -> p t n", t=PACK))
+        wv_raw = consts.tile([P, PACK, UP_COLS // 2], BF16)
+        nc.sync.dma_start(out=wv_raw[:], in_=W_v_up.rearrange("(p t) n -> p t n", t=PACK))
         cos_raw = consts.tile([P, POSITIONS, PAIRS], BF16)
         nc.sync.dma_start(out=cos_raw[:], in_=rope_cos.rearrange("(p t) i -> p t i", t=POSITIONS))
+        load_chunk(2)
         sin_raw = consts.tile([P, POSITIONS, PAIRS], BF16)
         nc.sync.dma_start(out=sin_raw[:], in_=rope_sin.rearrange("(p t) i -> p t i", t=POSITIONS))
-        wup_raw = consts.tile([P, PACK, UP_COLS], BF16)
-        nc.sync.dma_start(out=wup_raw[:, :, 0 : UP_COLS // 2], in_=W_k_up.rearrange("(p t) n -> p t n", t=PACK))
-        nc.sync.dma_start(out=wup_raw[:, :, UP_COLS // 2 : UP_COLS], in_=W_v_up.rearrange("(p t) n -> p t n", t=PACK))
-        for c in range(2, N_CHUNKS):
+        for c in range(3, N_CHUNKS):
             load_chunk(c)
 
         ident = consts.tile([P, P], F32)
@@ -229,7 +231,7 @@ def tile_multiheadlatentattention_pb_t_kernel(
             if not live(c):
                 return
             b, first = place(c)
-            if c == N_CHUNKS - 1:
+            if c >= N_CHUNKS:
                 lo, hi = half * CHUNK // 2, (half + 1) * CHUNK // 2
             elif half == 1:
                 lo, hi = 0, CHUNK
@@ -255,7 +257,9 @@ def tile_multiheadlatentattention_pb_t_kernel(
             store(s, 1)
 
         wd_grouped = consts.tile([P, PACK, P, PACK], BF16, align_bytes=64)
-        nc.vector.tensor_copy(out=wd_grouped[:], in_=wd_raw[:].rearrange("p t (m f) -> p f m t", f=PACK))
+        wd_raw_by_f = wd_raw[:].rearrange("p t (m f) -> p f m t", f=PACK)
+        nc.vector.tensor_copy(out=wd_grouped[:, 0:2], in_=wd_raw_by_f[:, 0:2])
+        nc.scalar.copy(out=wd_grouped[:, 2:4], in_=wd_raw_by_f[:, 2:4])
         wd_codes, wd_scales = quantise("wd", wd_grouped[:].rearrange("p f m t -> p (f m t)"), D_LATENT, consts)
         wr_grouped = consts.tile([P, ROPE_COLS, PACK], BF16, align_bytes=64)
         for h in range(HEADS):
@@ -268,19 +272,17 @@ def tile_multiheadlatentattention_pb_t_kernel(
         wr_codes, wr_scales = quantise("wr", wr_grouped[:].rearrange("p n t -> p (n t)"), ROPE_COLS, consts)
         step(-2)
         sin_signed = consts.tile([P, POSITIONS, 2, PAIRS], BF16)
+        wup_grouped = consts.tile([P, UP_COLS, PACK], BF16, align_bytes=64)
+        for side, raw in enumerate((wk_raw, wv_raw)):
+            for half in range(2):
+                cols = slice(half * P, (half + 1) * P)
+                to = (2 * side + half) * P
+                nc.scalar.copy(
+                    out=wup_grouped[:, to : to + P, :], in_=raw[:, :, cols].rearrange("p t n -> p n t")
+                )
+        step(-1)
         nc.vector.tensor_scalar(out=sin_signed[:, :, 0, :], in0=sin_raw[:], scalar1=-1.0, scalar2=None, op0=MULT)
         nc.vector.tensor_copy(out=sin_signed[:, :, 1, :], in_=sin_raw[:])
-        wup_grouped = consts.tile([P, UP_COLS, PACK], BF16, align_bytes=64)
-        for cols in (slice(n, n + P) for n in range(0, UP_COLS, P)):
-            nc.gpsimd.tensor_scalar(
-                out=wup_grouped[:, cols, :],
-                in0=wup_raw[:, :, cols].rearrange("p t n -> p n t"),
-                scalar1=1.0,
-                scalar2=0.0,
-                op0=MULT,
-                op1=ADD,
-            )
-        step(-1)
         wup_codes, wup_scales = quantise("wup", wup_grouped[:].rearrange("p n t -> p (n t)"), UP_COLS, consts)
         for s in range(N_CHUNKS):
             step(s)

@@ -116,7 +116,7 @@ def tile_multiheadlatentattention_pb_t_kernel(
                     words = x_sb[c][:, 2 * pair + j, :].bitcast(F32)
                     for u in range(2):
                         nc.tensor.transpose(x_t[:, j, u, :], words[:, u * P : (u + 1) * P], ident[:])
-                copy_out(pair)(
+                copy_out(0 if c in (8,) else pair)(
                     out=grouped_words[:, 2 * pair : 2 * pair + 2], in_=x_t[:].rearrange("p j u w -> p j w u")
                 )
 
@@ -208,6 +208,15 @@ def tile_multiheadlatentattention_pb_t_kernel(
                 op=ADD,
             )
 
+        def sin_table(g):
+            if not 0 <= g < CHUNKS_PER_SEQ:
+                return
+            positions = slice(g * CHUNK, (g + 1) * CHUNK)
+            for e, sign in ((0, -1.0), (1, 1.0)):
+                nc.gpsimd.tensor_scalar(
+                    out=sin_signed[:, positions, e, :], in0=sin_raw[:, positions, :], scalar1=sign, scalar2=0.0, op0=MULT, op1=ADD
+                )
+
         def up(c, j):
             if not live(c):
                 return
@@ -244,6 +253,8 @@ def tile_multiheadlatentattention_pb_t_kernel(
             quantise_down(s)
             quantise_x(s + 2)
             rotate_sin(s)
+            if s >= 0:
+                sin_table(s + 2)
             rotate_cos(s + 1)
             for j in range(CHUNK):
                 down(s + 1, j)
@@ -277,12 +288,10 @@ def tile_multiheadlatentattention_pb_t_kernel(
             for half in range(2):
                 cols = slice(half * P, (half + 1) * P)
                 to = (2 * side + half) * P
-                nc.scalar.copy(
-                    out=wup_grouped[:, to : to + P, :], in_=raw[:, :, cols].rearrange("p t n -> p n t")
-                )
+                copy_out(half)(out=wup_grouped[:, to : to + P, :], in_=raw[:, :, cols].rearrange("p t n -> p n t"))
         step(-1)
-        nc.vector.tensor_scalar(out=sin_signed[:, :, 0, :], in0=sin_raw[:], scalar1=-1.0, scalar2=None, op0=MULT)
-        nc.vector.tensor_copy(out=sin_signed[:, :, 1, :], in_=sin_raw[:])
+        sin_table(0)
+        sin_table(1)
         wup_codes, wup_scales = quantise("wup", wup_grouped[:].rearrange("p n t -> p (n t)"), UP_COLS, consts)
         for s in range(N_CHUNKS):
             step(s)

from contextlib import ExitStack

import concourse.mybir as mybir
from concourse.masks import make_identity

F32 = mybir.dt.float32
BF16 = mybir.dt.bfloat16
U32 = mybir.dt.uint32
U8 = mybir.dt.uint8
FP8X4 = mybir.dt.float8_e4m3fn_x4
MULT = mybir.AluOpType.mult
ADD = mybir.AluOpType.add

P = 128
PACK = 4
PSUM_BANKS = 8
BATCH, SEQ, D_MODEL = 2, 4096, 512
HEADS, D_HEAD, D_ROPE, D_LATENT = 2, 128, 64, 512
PAIRS = D_ROPE // 2
D_KEY = D_HEAD + D_ROPE
POSITIONS = SEQ // P
CHUNK = 4
CHUNK_TOKENS = CHUNK * P
CHUNKS_PER_SEQ = POSITIONS // CHUNK
N_CHUNKS = BATCH * CHUNKS_PER_SEQ
RUN = 4
UP_COLS = 2 * HEADS * D_HEAD
ROPE_COLS = HEADS * D_ROPE

assert D_MODEL == P * PACK and D_LATENT == P * PACK

FLOPS = 2 * BATCH * SEQ * (D_MODEL * D_LATENT + D_LATENT * UP_COLS + D_MODEL * ROPE_COLS)


def tile_multiheadlatentattention_pb_t_kernel(
    tc, x, W_kv_down, W_k_up, W_v_up, W_k_rope, rope_cos, rope_sin, out_0, out_1
):
    nc = tc.nc

    x_view = x.rearrange("b (p t) d -> b p t d", t=POSITIONS)
    keys_view = out_0.rearrange("b h (p t) f -> b p h t f", t=POSITIONS)
    values_view = out_1.rearrange("b h (p t) f -> b p h t f", t=POSITIONS)

    with ExitStack() as ctx:
        ctx.enter_context(tc.manual_schedule())
        consts = ctx.enter_context(tc.tile_pool(name="consts", bufs=1))
        x_pool = ctx.enter_context(tc.tile_pool(name="x_pool", bufs=N_CHUNKS))
        grouped_pool = ctx.enter_context(tc.tile_pool(name="grouped_pool", bufs=2))
        codes_pool = ctx.enter_context(tc.tile_pool(name="codes_pool", bufs=3))
        rope_pool = ctx.enter_context(tc.tile_pool(name="rope_pool", bufs=2))
        keys_pool = ctx.enter_context(tc.tile_pool(name="keys_pool", bufs=8))
        values_pool = ctx.enter_context(tc.tile_pool(name="values_pool", bufs=8))
        psum_k_r = ctx.enter_context(tc.psum_pool(name="psum_k_r", bufs=2))
        psum = ctx.enter_context(tc.psum_pool(name="psum", bufs=PSUM_BANKS - 2))

        x_sb, x_grouped, x_codes, x_scales = {}, {}, {}, {}
        d_grouped, d_codes, d_scales = {}, {}, {}
        k_r_banks, k_sb, v_sb = {}, {}, {}
        by_cos_tiles = {}

        def live(c):
            return 0 <= c < N_CHUNKS

        def copy_out(piece):
            return nc.scalar.copy if piece % 2 == 0 else nc.vector.tensor_copy

        def place(c):
            return c // CHUNKS_PER_SEQ, (c % CHUNKS_PER_SEQ) * CHUNK

        def load_chunk(c):
            b, first = place(c)
            x_sb[c] = x_pool.tile([P, CHUNK, D_MODEL], BF16, name="x_sb")
            nc.sync.dma_start(out=x_sb[c][:], in_=x_view[b, :, first : first + CHUNK, :])

        def quantise(name, grouped, width, pool):
            codes = pool.tile([P, width], U32, name=name + "_codes", align_bytes=64)
            scales = pool.tile([P, width], U8, name=name + "_scales", align_bytes=64)
            nc.vector.quantize_mx(out=codes[:].bitcast(FP8X4), scales=scales[:], in_=grouped)
            return codes, scales

        wd_raw = consts.tile([P, PACK, D_LATENT], BF16)
        nc.sync.dma_start(
            out=wd_raw[:].rearrange("p (u e) n -> p u e n", u=2),
            in_=W_kv_down.rearrange("(u p e) n -> p u e n", u=2, e=2),
        )
        load_chunk(0)
        wr_raw = consts.tile([P, PACK, ROPE_COLS], BF16)
        nc.sync.dma_start(
            out=wr_raw[:].rearrange("p (u e) n -> p u e n", u=2),
            in_=W_k_rope.rearrange("(u p e) n -> p u e n", u=2, e=2),
        )
        load_chunk(1)
        wk_raw = consts.tile([P, PACK, UP_COLS // 2], BF16)
        nc.sync.dma_start(out=wk_raw[:], in_=W_k_up.rearrange("(p t) n -> p t n", t=PACK))
        wv_raw = consts.tile([P, PACK, UP_COLS // 2], BF16)
        nc.sync.dma_start(out=wv_raw[:], in_=W_v_up.rearrange("(p t) n -> p t n", t=PACK))
        cos_raw = consts.tile([P, POSITIONS, PAIRS], BF16)
        nc.sync.dma_start(out=cos_raw[:], in_=rope_cos.rearrange("(p t) i -> p t i", t=POSITIONS))
        load_chunk(2)
        sin_raw = consts.tile([P, POSITIONS, PAIRS], BF16)
        nc.sync.dma_start(out=sin_raw[:], in_=rope_sin.rearrange("(p t) i -> p t i", t=POSITIONS))
        for c in range(3, N_CHUNKS):
            load_chunk(c)

        ident = consts.tile([P, P], F32)
        make_identity(nc, ident[:])

        def transpose_chunk(c):
            if not live(c):
                return
            x_grouped[c] = grouped_pool.tile([P, CHUNK_TOKENS * PACK], BF16, name="x_grouped", align_bytes=64)
            grouped_words = x_grouped[c][:].bitcast(F32).rearrange("p (j w u) -> p j w u", j=CHUNK, u=2)
            for pair in range(CHUNK // 2):
                x_t = psum.tile([P, 2, 2, P], F32, name="x_t", tag="bank")
                for j in range(2):
                    words = x_sb[c][:, 2 * pair + j, :].bitcast(F32)
                    for u in range(2):
                        nc.tensor.transpose(x_t[:, j, u, :], words[:, u * P : (u + 1) * P], ident[:])
                copy_out(0 if c in (8,) else pair)(
                    out=grouped_words[:, 2 * pair : 2 * pair + 2], in_=x_t[:].rearrange("p j u w -> p j w u")
                )

        def quantise_x(c):
            if not live(c):
                return
            x_codes[c], x_scales[c] = quantise("x", x_grouped[c][:], CHUNK_TOKENS, codes_pool)

        def down(c, j):
            if not live(c):
                return
            if j == 0:
                d_grouped[c] = grouped_pool.tile([P, CHUNK, P, PACK], BF16, name="d_grouped", align_bytes=64)
            tokens = slice(j * P, (j + 1) * P)
            down_t = psum.tile([P, PACK, P], F32, name="down_t", tag="bank")
            for f in range(PACK):
                cols = slice(f * P, (f + 1) * P)
                nc.tensor.matmul_mx(
                    out=down_t[:, f, :],
                    lhsT=wd_codes[:, cols].bitcast(FP8X4),
                    lhsT_scale=wd_scales[:, cols],
                    rhs=x_codes[c][:, tokens].bitcast(FP8X4),
                    rhs_scale=x_scales[c][:, tokens],
                    start=True,
                    stop=True,
                )
            nc.scalar.copy(
                out=d_grouped[c][:, j].rearrange("p (g i) f -> p g f i", i=RUN),
                in_=down_t[:].rearrange("p f (g i) -> p g f i", i=RUN),
            )

        def quantise_down(c):
            if not live(c):
                return
            d_codes[c], d_scales[c] = quantise(
                "d", d_grouped[c][:].rearrange("p j w f -> p (j w f)"), CHUNK_TOKENS, codes_pool
            )

        def rope_products(c):
            if not live(c):
                return
            k_r = psum_k_r.tile([P, CHUNK, ROPE_COLS], F32, name="k_r")
            k_r_banks[c] = k_r
            for j in range(CHUNK):
                tokens = slice(j * P, (j + 1) * P)
                nc.tensor.matmul_mx(
                    out=k_r[:, j, :],
                    lhsT=x_codes[c][:, tokens].bitcast(FP8X4),
                    lhsT_scale=x_scales[c][:, tokens],
                    rhs=wr_codes[:].bitcast(FP8X4),
                    rhs_scale=wr_scales[:],
                    start=True,
                    stop=True,
                )

        def rotate_cos(c):
            if not live(c):
                return
            first = place(c)[1]
            positions = slice(first, first + CHUNK)
            k_r = k_r_banks[c]
            k_sb[c] = keys_pool.tile([P, HEADS, CHUNK, D_KEY], F32, name="k_sb")
            by_cos = rope_pool.tile([P, CHUNK, 2 * HEADS, PAIRS], F32, name="by_cos")
            by_cos_tiles[c] = by_cos
            nc.vector.tensor_tensor(
                out=by_cos[:],
                in0=k_r[:].rearrange("p j (g i) -> p j g i", i=PAIRS),
                in1=cos_raw[:, positions, :].unsqueeze(2).to_broadcast([P, CHUNK, 2 * HEADS, PAIRS]),
                op=MULT,
            )
        def rotate_sin(c):
            if not live(c):
                return
            first = place(c)[1]
            positions = slice(first, first + CHUNK)
            k_r = k_r_banks[c]
            by_cos = by_cos_tiles[c]
            by_sin = rope_pool.tile([P, CHUNK, HEADS, 2, PAIRS], F32, name="by_sin")
            nc.vector.tensor_tensor(
                out=by_sin[:],
                in0=k_r[:].rearrange("p j (h e i) -> p j h e i", h=HEADS, e=2)[:, :, :, ::-1, :],
                in1=sin_signed[:, positions].unsqueeze(2).to_broadcast([P, CHUNK, HEADS, 2, PAIRS]),
                op=MULT,
            )
            nc.gpsimd.tensor_tensor(
                out=k_sb[c][:, :, :, D_HEAD:D_KEY].rearrange("p h j (i e) -> p j h i e", e=2),
                in0=by_cos[:].rearrange("p j (h e) i -> p j h i e", e=2),
                in1=by_sin[:].rearrange("p j h e i -> p j h i e"),
                op=ADD,
            )

        def sin_table(g):
            if not 0 <= g < CHUNKS_PER_SEQ:
                return
            positions = slice(g * CHUNK, (g + 1) * CHUNK)
            for e, sign in ((0, -1.0), (1, 1.0)):
                nc.gpsimd.tensor_scalar(
                    out=sin_signed[:, positions, e, :], in0=sin_raw[:, positions, :], scalar1=sign, scalar2=0.0, op0=MULT, op1=ADD
                )

        def up(c, j):
            if not live(c):
                return
            if j == 0:
                v_sb[c] = values_pool.tile([P, HEADS, CHUNK, D_HEAD], F32, name="v_sb")
            tokens = slice(j * P, (j + 1) * P)
            kc_v = psum.tile([P, 2, HEADS, D_HEAD], F32, name="kc_v", tag="bank")
            nc.tensor.matmul_mx(
                out=kc_v[:].rearrange("p s h f -> p (s h f)"),
                lhsT=d_codes[c][:, tokens].bitcast(FP8X4),
                lhsT_scale=d_scales[c][:, tokens],
                rhs=wup_codes[:].bitcast(FP8X4),
                rhs_scale=wup_scales[:],
                start=True,
                stop=True,
            )
            copy_out(j)(out=k_sb[c][:, :, j, 0:D_HEAD], in_=kc_v[:, 0])
            copy_out(j)(out=v_sb[c][:, :, j, :], in_=kc_v[:, 1])

        def store(c, half):
            if not live(c):
                return
            b, first = place(c)
            if c >= N_CHUNKS:
                lo, hi = half * CHUNK // 2, (half + 1) * CHUNK // 2
            elif half == 1:
                lo, hi = 0, CHUNK
            else:
                return
            nc.sync.dma_start(out=keys_view[b, :, :, first + lo : first + hi, :], in_=k_sb[c][:, :, lo:hi, :])
            nc.sync.dma_start(out=values_view[b, :, :, first + lo : first + hi, :], in_=v_sb[c][:, :, lo:hi, :])

        def step(s):
            quantise_down(s)
            quantise_x(s + 2)
            rotate_sin(s)
            if s >= 0:
                sin_table(s + 2)
            rotate_cos(s + 1)
            for j in range(CHUNK):
                down(s + 1, j)
            transpose_chunk(s + 3)
            up(s, 0)
            up(s, 1)
            store(s, 0)
            up(s, 2)
            up(s, 3)
            rope_products(s + 2)
            store(s, 1)

        wd_grouped = consts.tile([P, PACK, P, PACK], BF16, align_bytes=64)
        wd_raw_by_f = wd_raw[:].rearrange("p t (m f) -> p f m t", f=PACK)
        nc.vector.tensor_copy(out=wd_grouped[:, 0:2], in_=wd_raw_by_f[:, 0:2])
        nc.scalar.copy(out=wd_grouped[:, 2:4], in_=wd_raw_by_f[:, 2:4])
        wd_codes, wd_scales = quantise("wd", wd_grouped[:].rearrange("p f m t -> p (f m t)"), D_LATENT, consts)
        wr_grouped = consts.tile([P, ROPE_COLS, PACK], BF16, align_bytes=64)
        for h in range(HEADS):
            cols = slice(h * D_ROPE, (h + 1) * D_ROPE)
            nc.scalar.copy(
                out=wr_grouped[:, cols, :].rearrange("p (e i) t -> p e i t", e=2),
                in_=wr_raw[:, :, cols].rearrange("p t (i e) -> p e i t", e=2),
            )
        step(-3)
        wr_codes, wr_scales = quantise("wr", wr_grouped[:].rearrange("p n t -> p (n t)"), ROPE_COLS, consts)
        step(-2)
        sin_signed = consts.tile([P, POSITIONS, 2, PAIRS], BF16)
        wup_grouped = consts.tile([P, UP_COLS, PACK], BF16, align_bytes=64)
        for side, raw in enumerate((wk_raw, wv_raw)):
            for half in range(2):
                cols = slice(half * P, (half + 1) * P)
                to = (2 * side + half) * P
                copy_out(half)(out=wup_grouped[:, to : to + P, :], in_=raw[:, :, cols].rearrange("p t n -> p n t"))
        step(-1)
        sin_table(0)
        sin_table(1)
        wup_codes, wup_scales = quantise("wup", wup_grouped[:].rearrange("p n t -> p (n t)"), UP_COLS, consts)
        for s in range(N_CHUNKS):
            step(s)
